import numpy as np
import ml_dtypes

BF16 = ml_dtypes.bfloat16


def bf(x):
    return np.asarray(x, np.float32).astype(BF16)


def f32(x):
    return np.asarray(x, np.float32)


def f64(x):
    return np.asarray(x).astype(np.float64)


def striped(idx):
    return np.tile(idx.reshape(-1, 16).T, (8, 1))


V, D, H, H2, NC, B, T, N = 512, 128, 512, 256, 128, 128, 8, 1024
EPS = 1e-5
A1, A2, A3 = 0.25, 0.0625, 0.0625
TERMS = 150
LIM = 6.0


def erf(a):
    c = np.clip(a, -LIM, LIM)
    term = c.copy()
    total = c.copy()
    for n in range(1, TERMS):
        term = term * 2.0 * c * c / (2.0 * n + 1.0)
        total = total + term
    val = 2.0 / np.sqrt(np.pi) * np.exp(-c * c) * total
    return np.where(np.abs(a) > LIM, np.sign(a), val)


def gelu_erf(a):
    return 0.5 * a * (1.0 + erf(a / np.sqrt(2.0)))


def layer_norm(a, gain, beta):
    mu = a.mean(axis=0, keepdims=True)
    var = ((a - mu) ** 2).mean(axis=0, keepdims=True)
    return (a - mu) / np.sqrt(var + EPS) * gain + beta


def signs(shape, amp):
    return bf(np.where(np.random.random(shape) < 0.5, -amp, amp))


def setup_inputs():
    return {"table": bf(np.random.standard_normal((D, V))), "w1": signs((D, H), A1), "b1": f32(0.1 * np.random.standard_normal((H, 1))), "gain1": f32(1.0 + 0.1 * np.random.standard_normal((H, 1))), "beta1": f32(0.1 * np.random.standard_normal((H, 1))), "w2": signs((H, H2), A2), "b2": f32(0.1 * np.random.standard_normal((H2, 1))), "gain2": f32(1.0 + 0.1 * np.random.standard_normal((H2, 1))), "beta2": f32(0.1 * np.random.standard_normal((H2, 1))), "w3": signs((H2, NC), A3), "b3": f32(0.1 * np.random.standard_normal((NC, 1))), "offs": striped(np.random.permutation(np.tile(np.arange(V), 2))[:N])}


def reference(table, w1, b1, gain1, beta1, w2, b2, gain2, beta2, w3, b3, offs):
    idx = offs[:16].T.reshape(-1)
    proj = f64(w1).T @ f64(table)[:, idx]
    u = proj.reshape(H, B, T).sum(axis=2) / T + f64(b1)
    h1 = gelu_erf(layer_norm(u, f64(gain1), f64(beta1)))
    v = f64(w2).T @ h1 + f64(b2)
    h2 = gelu_erf(layer_norm(v, f64(gain2), f64(beta2)))
    return f64(w3).T @ h2 + f64(b3)

@@ -1,0 +1,146 @@
+import concourse.mybir as mybir
+from concourse.masks import make_identity
+
+BF16, F32, U16 = mybir.dt.bfloat16, mybir.dt.float32, mybir.dt.uint16
+ALU = mybir.AluOpType
+ACT = mybir.ActivationFunctionType
+
+P = 128
+V, D, H, H2, NC, B, T, N = 512, 128, 512, 256, 128, 128, 8, 1024
+EPS = 1e-5
+H_BLOCKS = H // P
+H2_BLOCKS = H2 // P
+PIECE = 512
+PIECES = N // PIECE
+SAMPLES = PIECE // T
+
+
+FLOPS = 2 * D * H * N + 2 * H * H2 * B + 2 * H2 * NC * B
+
+
+def load_columns(nc, pool, vector, name):
+    columns = pool.tile([P, vector.shape[0] // P], F32, name=name)
+    with nc.allow_non_contiguous_dma(reason="4-byte elements, one to a partition"):
+        nc.scalar.dma_start(columns[:], vector.rearrange("(c p) o -> p (c o)", p=P))
+    return columns
+
+
+def normalise(nc, work, x_ps, eps, minus_half, layer):
+    stats = work.tile([P, 6], F32, name=f"stats{layer}")
+    nc.vector.bn_stats(stats[:], x_ps[:])
+    mean_var = work.tile([P, 2], F32, name=f"mean_var{layer}")
+    nc.vector.bn_aggr(mean_var[:], stats[:])
+    var_eps = work.tile([P, 1], F32, name=f"var_eps{layer}")
+    nc.vector.tensor_scalar_add(var_eps[:], mean_var[:, 1:2], eps)
+    rstd = work.tile([P, 1], F32, name=f"rstd{layer}")
+    nc.gpsimd.tensor_tensor(rstd[:], var_eps[:], minus_half[:], ALU.pow)
+    normed = work.tile(list(x_ps.shape), F32, name=f"normed{layer}")
+    nc.vector.tensor_scalar(normed[:], x_ps[:], mean_var[:, 0:1], rstd[:], ALU.subtract, ALU.mult)
+    return normed
+
+
+def gelu_of_affine(nc, flipped, work, normed, identity, gain, beta, layer):
+    blocks = gain.shape[1]
+    h = work.tile([P, blocks, B], BF16, name=f"h{layer}")
+    for c in range(blocks):
+        x_ps = flipped.tile([P, B], F32, name="x_ps")
+        nc.tensor.transpose(x_ps[:], normed[:, c * P : (c + 1) * P], identity[:])
+        nc.scalar.activation(
+            h[:, c, :],
+            x_ps[:],
+            ACT.Gelu,
+            bias=beta[:, c : c + 1],
+            scale=gain[:, c : c + 1],
+        )
+    return h
+
+
+def tile_ternarycreditrisknet_kernel(
+    tc, table, w1, b1, gain1, beta1, w2, b2, gain2, beta2, w3, b3, offs, out
+):
+    nc = tc.nc
+    with (
+        tc.tile_pool(name="held", bufs=1) as held,
+        tc.tile_pool(name="work", bufs=1) as work,
+        tc.psum_pool(name="sums", bufs=1) as sums,
+    ):
+        offsets = held.tile([P, N // 16], U16, name="offsets")
+        nc.sync.dma_start(offsets[:], offs)
+        table_sb = held.tile([D, V], BF16, name="table_sb")
+        nc.sync.dma_start(table_sb[:], table)
+        w1_sb = held.tile([D, H], BF16, name="w1_sb")
+        nc.scalar.dma_start(w1_sb[:], w1)
+
+        b1_sb = load_columns(nc, held, b1, "b1_sb")
+        gain1_sb = load_columns(nc, held, gain1, "gain1_sb")
+        beta1_sb = load_columns(nc, held, beta1, "beta1_sb")
+        gain2_sb = load_columns(nc, held, gain2, "gain2_sb")
+        beta2_sb = load_columns(nc, held, beta2, "beta2_sb")
+        b3_sb = load_columns(nc, held, b3, "b3_sb")
+
+        identity = held.tile([P, P], F32, name="identity")
+        make_identity(nc, identity[:])
+        ones = held.tile([1, B], F32, name="ones")
+        nc.vector.memset(ones[:], 1.0)
+        minus_half = held.tile([P, 1], F32, name="minus_half")
+        nc.vector.memset(minus_half[:], -0.5)
+
+        w2_sb = held.tile([P, H_BLOCKS, H2], BF16, name="w2_sb")
+        nc.gpsimd.dma_start(w2_sb[:], w2.rearrange("(c p) n -> p c n", p=P))
+        w3_sb = held.tile([P, H2_BLOCKS, NC], BF16, name="w3_sb")
+        nc.gpsimd.dma_start(w3_sb[:], w3.rearrange("(c p) q -> p c q", p=P))
+        b2_row = held.tile([1, H2], F32, name="b2_row")
+        nc.gpsimd.dma_start(b2_row[:], b2.rearrange("h o -> o h"))
+
+        warm = work.tile([P, 1], F32, name="warm")
+        nc.scalar.activation(warm[:], minus_half[:], ACT.Gelu)
+
+        token_sum = work.tile([P, H_BLOCKS, B], F32, name="token_sum")
+        u = work.tile([P, H_BLOCKS, B], F32, name="u")
+        with tc.psum_pool(name="proj", bufs=4) as proj:
+            for c in range(H_BLOCKS):
+                for piece in range(PIECES):
+                    p_ps = proj.tile([P, PIECE], F32, name="p_ps")
+                    piece_offsets = offsets[:, piece * (PIECE // 16) : (piece + 1) * (PIECE // 16)]
+                    nc.tensor.matmul(
+                        p_ps[:],
+                        lhsT=w1_sb[:, c * P : (c + 1) * P],
+                        rhs=table_sb[:].indirect(piece_offsets),
+                        start=True,
+                        stop=True,
+                    )
+                    nc.vector.tensor_reduce(
+                        out=token_sum[:, c, piece * SAMPLES : (piece + 1) * SAMPLES],
+                        in_=p_ps[:].rearrange("p (i t) -> p i t", t=T),
+                        axis=mybir.AxisListType.X,
+                        op=ALU.add,
+                    )
+                nc.scalar.activation(
+                    u[:, c, :], token_sum[:, c, :], ACT.Identity, bias=b1_sb[:, c : c + 1], scale=1.0 / T
+                )
+
+        v_ps = sums.tile([B, H2], F32, name="v_ps")
+        nc.tensor.matmul(v_ps[:], lhsT=ones[:], rhs=b2_row[:], start=True, stop=False)
+
+        with tc.psum_pool(name="flipped", bufs=4) as flipped:
+            u_ps = sums.tile([B, H], F32, name="u_ps")
+            for c in range(H_BLOCKS):
+                nc.tensor.transpose(u_ps[:, c * P : (c + 1) * P], u[:, c, :], identity[:])
+            normed1 = normalise(nc, work, u_ps, EPS, minus_half, 1)
+            h1 = gelu_of_affine(nc, flipped, work, normed1, identity, gain1_sb, beta1_sb, 1)
+
+            for c in range(H_BLOCKS):
+                nc.tensor.matmul(
+                    v_ps[:], lhsT=h1[:, c, :], rhs=w2_sb[:, c, :], start=False, stop=(c == H_BLOCKS - 1)
+                )
+            normed2 = normalise(nc, work, v_ps, EPS, minus_half, 2)
+            h2 = gelu_of_affine(nc, flipped, work, normed2, identity, gain2_sb, beta2_sb, 2)
+
+            out_ps = sums.tile([NC, B], F32, name="out_ps")
+            for c in range(H2_BLOCKS):
+                nc.tensor.matmul(
+                    out_ps[:], lhsT=w3_sb[:, c, :], rhs=h2[:, c, :], start=(c == 0), stop=(c == H2_BLOCKS - 1)
+                )
+            out_sb = work.tile([NC, B], F32, name="out_sb")
+            nc.vector.tensor_scalar_add(out_sb[:], out_ps[:], b3_sb[:])
+            nc.sync.dma_start(out, out_sb[:])

@@ -25,15 +25,13 @@ def load_columns(nc, pool, vector, name):
     return columns
 
 
-def normalise(nc, work, x_ps, eps, minus_half, layer):
+def normalise(nc, work, x_ps, eps, layer):
     stats = work.tile([P, 6], F32, name=f"stats{layer}")
     nc.vector.bn_stats(stats[:], x_ps[:])
     mean_var = work.tile([P, 2], F32, name=f"mean_var{layer}")
     nc.vector.bn_aggr(mean_var[:], stats[:])
-    var_eps = work.tile([P, 1], F32, name=f"var_eps{layer}")
-    nc.vector.tensor_scalar_add(var_eps[:], mean_var[:, 1:2], eps)
     rstd = work.tile([P, 1], F32, name=f"rstd{layer}")
-    nc.gpsimd.tensor_tensor(rstd[:], var_eps[:], minus_half[:], ALU.pow)
+    nc.scalar.activation(rstd[:], mean_var[:, 1:2], ACT.Abs_reciprocal_sqrt, bias=eps)
     normed = work.tile(list(x_ps.shape), F32, name=f"normed{layer}")
     nc.vector.tensor_scalar(normed[:], x_ps[:], mean_var[:, 0:1], rstd[:], ALU.subtract, ALU.mult)
     return normed
@@ -82,8 +80,6 @@ def tile_ternarycreditrisknet_kernel(
         make_identity(nc, identity[:])
         ones = held.tile([1, B], F32, name="ones")
         nc.vector.memset(ones[:], 1.0)
-        minus_half = held.tile([P, 1], F32, name="minus_half")
-        nc.vector.memset(minus_half[:], -0.5)
 
         w2_sb = held.tile([P, H_BLOCKS, H2], BF16, name="w2_sb")
         nc.gpsimd.dma_start(w2_sb[:], w2.rearrange("(c p) n -> p c n", p=P))
@@ -92,8 +88,10 @@ def tile_ternarycreditrisknet_kernel(
         b2_row = held.tile([1, H2], F32, name="b2_row")
         nc.gpsimd.dma_start(b2_row[:], b2.rearrange("h o -> o h"))
 
+        one = held.tile([P, 1], F32, name="one")
+        nc.vector.memset(one[:], 1.0)
         warm = work.tile([P, 1], F32, name="warm")
-        nc.scalar.activation(warm[:], minus_half[:], ACT.Gelu)
+        nc.scalar.activation(warm[:], one[:], ACT.Abs_reciprocal_sqrt)
 
         token_sum = work.tile([P, H_BLOCKS, B], F32, name="token_sum")
         u = work.tile([P, H_BLOCKS, B], F32, name="u")
@@ -126,14 +124,14 @@ def tile_ternarycreditrisknet_kernel(
             u_ps = sums.tile([B, H], F32, name="u_ps")
             for c in range(H_BLOCKS):
                 nc.tensor.transpose(u_ps[:, c * P : (c + 1) * P], u[:, c, :], identity[:])
-            normed1 = normalise(nc, work, u_ps, EPS, minus_half, 1)
+            normed1 = normalise(nc, work, u_ps, EPS, 1)
             h1 = gelu_of_affine(nc, flipped, work, normed1, identity, gain1_sb, beta1_sb, 1)
 
             for c in range(H_BLOCKS):
                 nc.tensor.matmul(
                     v_ps[:], lhsT=h1[:, c, :], rhs=w2_sb[:, c, :], start=False, stop=(c == H_BLOCKS - 1)
                 )
-            normed2 = normalise(nc, work, v_ps, EPS, minus_half, 2)
+            normed2 = normalise(nc, work, v_ps, EPS, 2)
             h2 = gelu_of_affine(nc, flipped, work, normed2, identity, gain2_sb, beta2_sb, 2)
 
             out_ps = sums.tile([NC, B], F32, name="out_ps")

@@ -13,6 +13,7 @@ H2_BLOCKS = H2 // P
 PIECE = 512
 PIECES = N // PIECE
 SAMPLES = PIECE // T
+WARM_MATMULS = 6
 
 
 FLOPS = 2 * D * H * N + 2 * H * H2 * B + 2 * H2 * NC * B
@@ -76,6 +77,8 @@ def tile_ternarycreditrisknet_kernel(
         beta2_sb = load_columns(nc, held, beta2, "beta2_sb")
         b3_sb = load_columns(nc, held, b3, "b3_sb")
 
+        zeros = held.tile([P, PIECE], BF16, name="zeros")
+        nc.vector.memset(zeros[:], 0.0)
         identity = held.tile([P, P], F32, name="identity")
         make_identity(nc, identity[:])
         ones = held.tile([1, B], F32, name="ones")
@@ -96,6 +99,9 @@ def tile_ternarycreditrisknet_kernel(
         token_sum = work.tile([P, H_BLOCKS, B], F32, name="token_sum")
         u = work.tile([P, H_BLOCKS, B], F32, name="u")
         with tc.psum_pool(name="proj", bufs=4) as proj:
+            for k in range(WARM_MATMULS):
+                p_ps = proj.tile([P, PIECE], F32, name="p_ps")
+                nc.tensor.matmul(p_ps[:], lhsT=zeros[:, 0:P], rhs=zeros[:], start=True, stop=True)
             for c in range(H_BLOCKS):
                 for piece in range(PIECES):
                     p_ps = proj.tile([P, PIECE], F32, name="p_ps")

@@ -13,8 +13,8 @@ H2_BLOCKS = H2 // P
 PIECE = 512
 PIECES = N // PIECE
 SAMPLES = PIECE // T
-WARM_MATMULS = 6
-
+STATS = 6
+BANKS = 6
 
 FLOPS = 2 * D * H * N + 2 * H * H2 * B + 2 * H2 * NC * B
 
@@ -22,35 +22,22 @@ FLOPS = 2 * D * H * N + 2 * H * H2 * B + 2 * H2 * NC * B
 def load_columns(nc, pool, vector, name):
     columns = pool.tile([P, vector.shape[0] // P], F32, name=name)
     with nc.allow_non_contiguous_dma(reason="4-byte elements, one to a partition"):
-        nc.scalar.dma_start(columns[:], vector.rearrange("(c p) o -> p (c o)", p=P))
+        nc.sync.dma_start(columns[:], vector.rearrange("(c p) o -> p (c o)", p=P))
     return columns
 
 
-def normalise(nc, work, x_ps, eps, layer):
-    stats = work.tile([P, 6], F32, name=f"stats{layer}")
-    nc.vector.bn_stats(stats[:], x_ps[:])
+def norm_gelu(nc, work, banks, x_blocks, stats, identity, gain, beta, layer):
     mean_var = work.tile([P, 2], F32, name=f"mean_var{layer}")
     nc.vector.bn_aggr(mean_var[:], stats[:])
     rstd = work.tile([P, 1], F32, name=f"rstd{layer}")
-    nc.scalar.activation(rstd[:], mean_var[:, 1:2], ACT.Abs_reciprocal_sqrt, bias=eps)
-    normed = work.tile(list(x_ps.shape), F32, name=f"normed{layer}")
-    nc.vector.tensor_scalar(normed[:], x_ps[:], mean_var[:, 0:1], rstd[:], ALU.subtract, ALU.mult)
-    return normed
-
-
-def gelu_of_affine(nc, flipped, work, normed, identity, gain, beta, layer):
-    blocks = gain.shape[1]
-    h = work.tile([P, blocks, B], BF16, name=f"h{layer}")
-    for c in range(blocks):
-        x_ps = flipped.tile([P, B], F32, name="x_ps")
-        nc.tensor.transpose(x_ps[:], normed[:, c * P : (c + 1) * P], identity[:])
-        nc.scalar.activation(
-            h[:, c, :],
-            x_ps[:],
-            ACT.Gelu,
-            bias=beta[:, c : c + 1],
-            scale=gain[:, c : c + 1],
-        )
+    nc.scalar.activation(rstd[:], mean_var[:, 1:2], ACT.Abs_reciprocal_sqrt, bias=EPS)
+    h = work.tile([P, len(x_blocks), B], BF16, name=f"h{layer}")
+    for c, x_block in enumerate(x_blocks):
+        normed = work.tile([B, P], F32, name=f"normed{layer}_{c}")
+        nc.vector.tensor_scalar(normed[:], x_block, mean_var[:, 0:1], rstd[:], ALU.subtract, ALU.mult)
+        flipped = banks.tile([P, B], F32, name="flipped", tag="bank")
+        nc.tensor.transpose(flipped[:], normed[:], identity[:])
+        nc.scalar.activation(h[:, c, :], flipped[:], ACT.Gelu, bias=beta[:, c : c + 1], scale=gain[:, c : c + 1])
     return h
 
 
@@ -61,35 +48,33 @@ def tile_ternarycreditrisknet_kernel(
     with (
         tc.tile_pool(name="held", bufs=1) as held,
         tc.tile_pool(name="work", bufs=1) as work,
+        tc.psum_pool(name="banks", bufs=BANKS) as banks,
         tc.psum_pool(name="sums", bufs=1) as sums,
     ):
-        offsets = held.tile([P, N // 16], U16, name="offsets")
-        nc.sync.dma_start(offsets[:], offs)
         table_sb = held.tile([D, V], BF16, name="table_sb")
         nc.sync.dma_start(table_sb[:], table)
         w1_sb = held.tile([D, H], BF16, name="w1_sb")
-        nc.scalar.dma_start(w1_sb[:], w1)
-
+        nc.scalar.dma_start(w1_sb[:, 0:P], w1[:, 0:P])
+        nc.scalar.dma_start(w1_sb[:, P:H], w1[:, P:H])
+        offsets = held.tile([P, N // 16], U16, name="offsets")
+        nc.sync.dma_start(offsets[:], offs)
         b1_sb = load_columns(nc, held, b1, "b1_sb")
         gain1_sb = load_columns(nc, held, gain1, "gain1_sb")
         beta1_sb = load_columns(nc, held, beta1, "beta1_sb")
+        w2_sb = held.tile([P, H_BLOCKS, H2], BF16, name="w2_sb")
+        nc.sync.dma_start(w2_sb[:], w2.rearrange("(c p) n -> p c n", p=P))
+        b2_row = held.tile([1, H2], F32, name="b2_row")
+        nc.sync.dma_start(b2_row[:], b2.rearrange("h o -> o h"))
         gain2_sb = load_columns(nc, held, gain2, "gain2_sb")
         beta2_sb = load_columns(nc, held, beta2, "beta2_sb")
+        w3_sb = held.tile([P, H2_BLOCKS, NC], BF16, name="w3_sb")
+        nc.sync.dma_start(w3_sb[:], w3.rearrange("(c p) q -> p c q", p=P))
         b3_sb = load_columns(nc, held, b3, "b3_sb")
 
-        zeros = held.tile([P, PIECE], BF16, name="zeros")
-        nc.vector.memset(zeros[:], 0.0)
         identity = held.tile([P, P], F32, name="identity")
         make_identity(nc, identity[:])
         ones = held.tile([1, B], F32, name="ones")
         nc.vector.memset(ones[:], 1.0)
-
-        w2_sb = held.tile([P, H_BLOCKS, H2], BF16, name="w2_sb")
-        nc.gpsimd.dma_start(w2_sb[:], w2.rearrange("(c p) n -> p c n", p=P))
-        w3_sb = held.tile([P, H2_BLOCKS, NC], BF16, name="w3_sb")
-        nc.gpsimd.dma_start(w3_sb[:], w3.rearrange("(c p) q -> p c q", p=P))
-        b2_row = held.tile([1, H2], F32, name="b2_row")
-        nc.gpsimd.dma_start(b2_row[:], b2.rearrange("h o -> o h"))
 
         one = held.tile([P, 1], F32, name="one")
         nc.vector.memset(one[:], 1.0)
@@ -98,53 +83,48 @@ def tile_ternarycreditrisknet_kernel(
 
         token_sum = work.tile([P, H_BLOCKS, B], F32, name="token_sum")
         u = work.tile([P, H_BLOCKS, B], F32, name="u")
-        with tc.psum_pool(name="proj", bufs=4) as proj:
-            for k in range(WARM_MATMULS):
-                p_ps = proj.tile([P, PIECE], F32, name="p_ps")
-                nc.tensor.matmul(p_ps[:], lhsT=zeros[:, 0:P], rhs=zeros[:], start=True, stop=True)
-            for c in range(H_BLOCKS):
-                for piece in range(PIECES):
-                    p_ps = proj.tile([P, PIECE], F32, name="p_ps")
-                    piece_offsets = offsets[:, piece * (PIECE // 16) : (piece + 1) * (PIECE // 16)]
-                    nc.tensor.matmul(
-                        p_ps[:],
-                        lhsT=w1_sb[:, c * P : (c + 1) * P],
-                        rhs=table_sb[:].indirect(piece_offsets),
-                        start=True,
-                        stop=True,
-                    )
-                    nc.vector.tensor_reduce(
-                        out=token_sum[:, c, piece * SAMPLES : (piece + 1) * SAMPLES],
-                        in_=p_ps[:].rearrange("p (i t) -> p i t", t=T),
-                        axis=mybir.AxisListType.X,
-                        op=ALU.add,
-                    )
-                nc.scalar.activation(
-                    u[:, c, :], token_sum[:, c, :], ACT.Identity, bias=b1_sb[:, c : c + 1], scale=1.0 / T
+        for c in range(H_BLOCKS):
+            for piece in range(PIECES):
+                p_ps = banks.tile([P, PIECE], F32, name="p_ps", tag="bank")
+                piece_offsets = offsets[:, piece * (PIECE // 16) : (piece + 1) * (PIECE // 16)]
+                nc.tensor.matmul(
+                    p_ps[:],
+                    lhsT=w1_sb[:, c * P : (c + 1) * P],
+                    rhs=table_sb[:].indirect(piece_offsets),
+                    start=True,
+                    stop=True,
                 )
+                nc.vector.tensor_reduce(
+                    out=token_sum[:, c, piece * SAMPLES : (piece + 1) * SAMPLES],
+                    in_=p_ps[:].rearrange("p (i t) -> p i t", t=T),
+                    axis=mybir.AxisListType.X,
+                    op=ALU.add,
+                )
+            nc.scalar.activation(
+                u[:, c, :], token_sum[:, c, :], ACT.Identity, bias=b1_sb[:, c : c + 1], scale=1.0 / T
+            )
+
+        u_blocks = []
+        stats1 = work.tile([P, H_BLOCKS * STATS], F32, name="stats1")
+        for c in range(H_BLOCKS):
+            u_ps = banks.tile([B, P], F32, name="u_ps", tag="bank")
+            nc.tensor.transpose(u_ps[:], u[:, c, :], identity[:])
+            nc.vector.bn_stats(stats1[:, c * STATS : (c + 1) * STATS], u_ps[:])
+            u_blocks.append(u_ps[:])
+        h1 = norm_gelu(nc, work, banks, u_blocks, stats1, identity, gain1_sb, beta1_sb, 1)
 
         v_ps = sums.tile([B, H2], F32, name="v_ps")
         nc.tensor.matmul(v_ps[:], lhsT=ones[:], rhs=b2_row[:], start=True, stop=False)
+        for c in range(H_BLOCKS):
+            nc.tensor.matmul(v_ps[:], lhsT=h1[:, c, :], rhs=w2_sb[:, c, :], start=False, stop=(c == H_BLOCKS - 1))
+        stats2 = work.tile([P, STATS], F32, name="stats2")
+        nc.vector.bn_stats(stats2[:], v_ps[:])
+        v_blocks = [v_ps[:, c * P : (c + 1) * P] for c in range(H2_BLOCKS)]
+        h2 = norm_gelu(nc, work, banks, v_blocks, stats2, identity, gain2_sb, beta2_sb, 2)
 
-        with tc.psum_pool(name="flipped", bufs=4) as flipped:
-            u_ps = sums.tile([B, H], F32, name="u_ps")
-            for c in range(H_BLOCKS):
-                nc.tensor.transpose(u_ps[:, c * P : (c + 1) * P], u[:, c, :], identity[:])
-            normed1 = normalise(nc, work, u_ps, EPS, 1)
-            h1 = gelu_of_affine(nc, flipped, work, normed1, identity, gain1_sb, beta1_sb, 1)
-
-            for c in range(H_BLOCKS):
-                nc.tensor.matmul(
-                    v_ps[:], lhsT=h1[:, c, :], rhs=w2_sb[:, c, :], start=False, stop=(c == H_BLOCKS - 1)
-                )
-            normed2 = normalise(nc, work, v_ps, EPS, 2)
-            h2 = gelu_of_affine(nc, flipped, work, normed2, identity, gain2_sb, beta2_sb, 2)
-
-            out_ps = sums.tile([NC, B], F32, name="out_ps")
-            for c in range(H2_BLOCKS):
-                nc.tensor.matmul(
-                    out_ps[:], lhsT=w3_sb[:, c, :], rhs=h2[:, c, :], start=(c == 0), stop=(c == H2_BLOCKS - 1)
-                )
-            out_sb = work.tile([NC, B], F32, name="out_sb")
-            nc.vector.tensor_scalar_add(out_sb[:], out_ps[:], b3_sb[:])
-            nc.sync.dma_start(out, out_sb[:])
+        out_ps = banks.tile([NC, B], F32, name="out_ps", tag="bank")
+        for c in range(H2_BLOCKS):
+            nc.tensor.matmul(out_ps[:], lhsT=w3_sb[:, c, :], rhs=h2[:, c, :], start=(c == 0), stop=(c == H2_BLOCKS - 1))
+        out_sb = work.tile([NC, B], F32, name="out_sb")
+        nc.vector.tensor_scalar_add(out_sb[:], out_ps[:], b3_sb[:])
+        nc.sync.dma_start(out, out_sb[:])

@@ -15,6 +15,7 @@ PIECES = N // PIECE
 SAMPLES = PIECE // T
 STATS = 6
 BANKS = 6
+WARM_MATMULS = 4
 
 FLOPS = 2 * D * H * N + 2 * H * H2 * B + 2 * H2 * NC * B
 
@@ -71,6 +72,8 @@ def tile_ternarycreditrisknet_kernel(
         nc.sync.dma_start(w3_sb[:], w3.rearrange("(c p) q -> p c q", p=P))
         b3_sb = load_columns(nc, held, b3, "b3_sb")
 
+        zeros = held.tile([P, PIECE], BF16, name="zeros")
+        nc.gpsimd.memset(zeros[:], 0.0)
         identity = held.tile([P, P], F32, name="identity")
         make_identity(nc, identity[:])
         ones = held.tile([1, B], F32, name="ones")
@@ -83,6 +86,9 @@ def tile_ternarycreditrisknet_kernel(
 
         token_sum = work.tile([P, H_BLOCKS, B], F32, name="token_sum")
         u = work.tile([P, H_BLOCKS, B], F32, name="u")
+        for k in range(WARM_MATMULS):
+            p_ps = banks.tile([P, PIECE], F32, name="p_ps", tag="bank")
+            nc.tensor.matmul(p_ps[:], lhsT=zeros[:, 0:P], rhs=zeros[:], start=True, stop=True)
         for c in range(H_BLOCKS):
             for piece in range(PIECES):
                 p_ps = banks.tile([P, PIECE], F32, name="p_ps", tag="bank")

@@ -15,16 +15,14 @@ PIECES = N // PIECE
 SAMPLES = PIECE // T
 STATS = 6
 BANKS = 6
-WARM_MATMULS = 4
+GAIN1, BETA1, GAIN2, BETA2, B3 = 0, 4, 8, 10, 12
+PARAM_COLUMNS = 13
 
 FLOPS = 2 * D * H * N + 2 * H * H2 * B + 2 * H2 * NC * B
 
 
-def load_columns(nc, pool, vector, name):
-    columns = pool.tile([P, vector.shape[0] // P], F32, name=name)
-    with nc.allow_non_contiguous_dma(reason="4-byte elements, one to a partition"):
-        nc.sync.dma_start(columns[:], vector.rearrange("(c p) o -> p (c o)", p=P))
-    return columns
+def rows_of(vector):
+    return vector.rearrange("(c p) o -> c (p o)", p=P)
 
 
 def norm_gelu(nc, work, banks, x_blocks, stats, identity, gain, beta, layer):
@@ -59,21 +57,20 @@ def tile_ternarycreditrisknet_kernel(
         nc.scalar.dma_start(w1_sb[:, P:H], w1[:, P:H])
         offsets = held.tile([P, N // 16], U16, name="offsets")
         nc.sync.dma_start(offsets[:], offs)
-        b1_sb = load_columns(nc, held, b1, "b1_sb")
-        gain1_sb = load_columns(nc, held, gain1, "gain1_sb")
-        beta1_sb = load_columns(nc, held, beta1, "beta1_sb")
+        b1_sb = held.tile([P, H_BLOCKS], F32, name="b1_sb")
+        with nc.allow_non_contiguous_dma(reason="4-byte elements, one to a partition"):
+            nc.scalar.dma_start(b1_sb[:], b1.rearrange("(c p) o -> p (c o)", p=P))
+        param_rows = held.tile([P, P], F32, name="param_rows")
+        nc.gpsimd.memset(param_rows[:], 0.0)
+        for vector, row in ((gain1, GAIN1), (beta1, BETA1), (gain2, GAIN2), (beta2, BETA2), (b3, B3)):
+            nc.sync.dma_start(param_rows[row : row + vector.shape[0] // P, :], rows_of(vector))
         w2_sb = held.tile([P, H_BLOCKS, H2], BF16, name="w2_sb")
         nc.sync.dma_start(w2_sb[:], w2.rearrange("(c p) n -> p c n", p=P))
         b2_row = held.tile([1, H2], F32, name="b2_row")
         nc.sync.dma_start(b2_row[:], b2.rearrange("h o -> o h"))
-        gain2_sb = load_columns(nc, held, gain2, "gain2_sb")
-        beta2_sb = load_columns(nc, held, beta2, "beta2_sb")
         w3_sb = held.tile([P, H2_BLOCKS, NC], BF16, name="w3_sb")
         nc.sync.dma_start(w3_sb[:], w3.rearrange("(c p) q -> p c q", p=P))
-        b3_sb = load_columns(nc, held, b3, "b3_sb")
 
-        zeros = held.tile([P, PIECE], BF16, name="zeros")
-        nc.gpsimd.memset(zeros[:], 0.0)
         identity = held.tile([P, P], F32, name="identity")
         make_identity(nc, identity[:])
         ones = held.tile([1, B], F32, name="ones")
@@ -86,9 +83,6 @@ def tile_ternarycreditrisknet_kernel(
 
         token_sum = work.tile([P, H_BLOCKS, B], F32, name="token_sum")
         u = work.tile([P, H_BLOCKS, B], F32, name="u")
-        for k in range(WARM_MATMULS):
-            p_ps = banks.tile([P, PIECE], F32, name="p_ps", tag="bank")
-            nc.tensor.matmul(p_ps[:], lhsT=zeros[:, 0:P], rhs=zeros[:], start=True, stop=True)
         for c in range(H_BLOCKS):
             for piece in range(PIECES):
                 p_ps = banks.tile([P, PIECE], F32, name="p_ps", tag="bank")
@@ -110,6 +104,11 @@ def tile_ternarycreditrisknet_kernel(
                 u[:, c, :], token_sum[:, c, :], ACT.Identity, bias=b1_sb[:, c : c + 1], scale=1.0 / T
             )
 
+        params_ps = banks.tile([P, P], F32, name="params_ps", tag="bank")
+        nc.tensor.transpose(params_ps[:], param_rows[:], identity[:])
+        params = held.tile([P, PARAM_COLUMNS], F32, name="params")
+        nc.scalar.copy(params[:], params_ps[:, 0:PARAM_COLUMNS])
+
         u_blocks = []
         stats1 = work.tile([P, H_BLOCKS * STATS], F32, name="stats1")
         for c in range(H_BLOCKS):
@@ -117,7 +116,7 @@ def tile_ternarycreditrisknet_kernel(
             nc.tensor.transpose(u_ps[:], u[:, c, :], identity[:])
             nc.vector.bn_stats(stats1[:, c * STATS : (c + 1) * STATS], u_ps[:])
             u_blocks.append(u_ps[:])
-        h1 = norm_gelu(nc, work, banks, u_blocks, stats1, identity, gain1_sb, beta1_sb, 1)
+        h1 = norm_gelu(nc, work, banks, u_blocks, stats1, identity, params[:, GAIN1:BETA1], params[:, BETA1:GAIN2], 1)
 
         v_ps = sums.tile([B, H2], F32, name="v_ps")
         nc.tensor.matmul(v_ps[:], lhsT=ones[:], rhs=b2_row[:], start=True, stop=False)
@@ -126,11 +125,11 @@ def tile_ternarycreditrisknet_kernel(
         stats2 = work.tile([P, STATS], F32, name="stats2")
         nc.vector.bn_stats(stats2[:], v_ps[:])
         v_blocks = [v_ps[:, c * P : (c + 1) * P] for c in range(H2_BLOCKS)]
-        h2 = norm_gelu(nc, work, banks, v_blocks, stats2, identity, gain2_sb, beta2_sb, 2)
+        h2 = norm_gelu(nc, work, banks, v_blocks, stats2, identity, params[:, GAIN2:BETA2], params[:, BETA2:B3], 2)
 
         out_ps = banks.tile([NC, B], F32, name="out_ps", tag="bank")
         for c in range(H2_BLOCKS):
             nc.tensor.matmul(out_ps[:], lhsT=w3_sb[:, c, :], rhs=h2[:, c, :], start=(c == 0), stop=(c == H2_BLOCKS - 1))
         out_sb = work.tile([NC, B], F32, name="out_sb")
-        nc.vector.tensor_scalar_add(out_sb[:], out_ps[:], b3_sb[:])
+        nc.vector.tensor_scalar_add(out_sb[:], out_ps[:], params[:, B3 : B3 + 1])
         nc.sync.dma_start(out, out_sb[:])

@@ -15,14 +15,15 @@ PIECES = N // PIECE
 SAMPLES = PIECE // T
 STATS = 6
 BANKS = 6
-GAIN1, BETA1, GAIN2, BETA2, B3 = 0, 4, 8, 10, 12
-PARAM_COLUMNS = 13
 
 FLOPS = 2 * D * H * N + 2 * H * H2 * B + 2 * H2 * NC * B
 
 
-def rows_of(vector):
-    return vector.rearrange("(c p) o -> c (p o)", p=P)
+def load_columns(nc, pool, vector, name):
+    columns = pool.tile([P, vector.shape[0] // P], F32, name=name)
+    with nc.allow_non_contiguous_dma(reason="4-byte elements, one to a partition"):
+        nc.sync.dma_start(columns[:], vector.rearrange("(c p) o -> p (c o)", p=P))
+    return columns
 
 
 def norm_gelu(nc, work, banks, x_blocks, stats, identity, gain, beta, layer):
@@ -53,23 +54,21 @@ def tile_ternarycreditrisknet_kernel(
         table_sb = held.tile([D, V], BF16, name="table_sb")
         nc.sync.dma_start(table_sb[:], table)
         w1_sb = held.tile([D, H], BF16, name="w1_sb")
-        nc.scalar.dma_start(w1_sb[:, 0:P], w1[:, 0:P])
-        nc.scalar.dma_start(w1_sb[:, P:H], w1[:, P:H])
+        nc.scalar.dma_start(w1_sb[:], w1)
         offsets = held.tile([P, N // 16], U16, name="offsets")
         nc.sync.dma_start(offsets[:], offs)
-        b1_sb = held.tile([P, H_BLOCKS], F32, name="b1_sb")
-        with nc.allow_non_contiguous_dma(reason="4-byte elements, one to a partition"):
-            nc.scalar.dma_start(b1_sb[:], b1.rearrange("(c p) o -> p (c o)", p=P))
-        param_rows = held.tile([P, P], F32, name="param_rows")
-        nc.gpsimd.memset(param_rows[:], 0.0)
-        for vector, row in ((gain1, GAIN1), (beta1, BETA1), (gain2, GAIN2), (beta2, BETA2), (b3, B3)):
-            nc.sync.dma_start(param_rows[row : row + vector.shape[0] // P, :], rows_of(vector))
+        b1_sb = load_columns(nc, held, b1, "b1_sb")
+        gain1_sb = load_columns(nc, held, gain1, "gain1_sb")
+        beta1_sb = load_columns(nc, held, beta1, "beta1_sb")
         w2_sb = held.tile([P, H_BLOCKS, H2], BF16, name="w2_sb")
         nc.sync.dma_start(w2_sb[:], w2.rearrange("(c p) n -> p c n", p=P))
         b2_row = held.tile([1, H2], F32, name="b2_row")
         nc.sync.dma_start(b2_row[:], b2.rearrange("h o -> o h"))
+        gain2_sb = load_columns(nc, held, gain2, "gain2_sb")
+        beta2_sb = load_columns(nc, held, beta2, "beta2_sb")
         w3_sb = held.tile([P, H2_BLOCKS, NC], BF16, name="w3_sb")
         nc.sync.dma_start(w3_sb[:], w3.rearrange("(c p) q -> p c q", p=P))
+        b3_sb = load_columns(nc, held, b3, "b3_sb")
 
         identity = held.tile([P, P], F32, name="identity")
         make_identity(nc, identity[:])
@@ -104,11 +103,6 @@ def tile_ternarycreditrisknet_kernel(
                 u[:, c, :], token_sum[:, c, :], ACT.Identity, bias=b1_sb[:, c : c + 1], scale=1.0 / T
             )
 
-        params_ps = banks.tile([P, P], F32, name="params_ps", tag="bank")
-        nc.tensor.transpose(params_ps[:], param_rows[:], identity[:])
-        params = held.tile([P, PARAM_COLUMNS], F32, name="params")
-        nc.scalar.copy(params[:], params_ps[:, 0:PARAM_COLUMNS])
-
         u_blocks = []
         stats1 = work.tile([P, H_BLOCKS * STATS], F32, name="stats1")
         for c in range(H_BLOCKS):
@@ -116,7 +110,7 @@ def tile_ternarycreditrisknet_kernel(
             nc.tensor.transpose(u_ps[:], u[:, c, :], identity[:])
             nc.vector.bn_stats(stats1[:, c * STATS : (c + 1) * STATS], u_ps[:])
             u_blocks.append(u_ps[:])
-        h1 = norm_gelu(nc, work, banks, u_blocks, stats1, identity, params[:, GAIN1:BETA1], params[:, BETA1:GAIN2], 1)
+        h1 = norm_gelu(nc, work, banks, u_blocks, stats1, identity, gain1_sb, beta1_sb, 1)
 
         v_ps = sums.tile([B, H2], F32, name="v_ps")
         nc.tensor.matmul(v_ps[:], lhsT=ones[:], rhs=b2_row[:], start=True, stop=False)
@@ -125,11 +119,11 @@ def tile_ternarycreditrisknet_kernel(
         stats2 = work.tile([P, STATS], F32, name="stats2")
         nc.vector.bn_stats(stats2[:], v_ps[:])
         v_blocks = [v_ps[:, c * P : (c + 1) * P] for c in range(H2_BLOCKS)]
-        h2 = norm_gelu(nc, work, banks, v_blocks, stats2, identity, params[:, GAIN2:BETA2], params[:, BETA2:B3], 2)
+        h2 = norm_gelu(nc, work, banks, v_blocks, stats2, identity, gain2_sb, beta2_sb, 2)
 
         out_ps = banks.tile([NC, B], F32, name="out_ps", tag="bank")
         for c in range(H2_BLOCKS):
             nc.tensor.matmul(out_ps[:], lhsT=w3_sb[:, c, :], rhs=h2[:, c, :], start=(c == 0), stop=(c == H2_BLOCKS - 1))
         out_sb = work.tile([NC, B], F32, name="out_sb")
-        nc.vector.tensor_scalar_add(out_sb[:], out_ps[:], params[:, B3 : B3 + 1])
+        nc.vector.tensor_scalar_add(out_sb[:], out_ps[:], b3_sb[:])
         nc.sync.dma_start(out, out_sb[:])

@@ -14,6 +14,7 @@ PIECE = 512
 PIECES = N // PIECE
 SAMPLES = PIECE // T
 STATS = 6
+TRIPLE = 3
 BANKS = 6
 
 FLOPS = 2 * D * H * N + 2 * H * H2 * B + 2 * H2 * NC * B
@@ -26,11 +27,18 @@ def load_columns(nc, pool, vector, name):
     return columns
 
 
-def norm_gelu(nc, work, banks, x_blocks, stats, identity, gain, beta, layer):
+def stats_tile(nc, work, chunks, features, layer):
+    stats = work.tile([P, chunks * STATS + TRIPLE], F32, name=f"stats{layer}")
+    nc.vector.memset(stats[:, chunks * STATS : chunks * STATS + 2], 0.0)
+    nc.vector.memset(stats[:, chunks * STATS + 2 : chunks * STATS + TRIPLE], features * EPS)
+    return stats
+
+
+def norm_gelu(nc, work, banks, x_blocks, stats, minus_half, identity, gain, beta, layer):
     mean_var = work.tile([P, 2], F32, name=f"mean_var{layer}")
     nc.vector.bn_aggr(mean_var[:], stats[:])
     rstd = work.tile([P, 1], F32, name=f"rstd{layer}")
-    nc.scalar.activation(rstd[:], mean_var[:, 1:2], ACT.Abs_reciprocal_sqrt, bias=EPS)
+    nc.gpsimd.tensor_tensor(rstd[:], mean_var[:, 1:2], minus_half[:], ALU.pow)
     h = work.tile([P, len(x_blocks), B], BF16, name=f"h{layer}")
     for c, x_block in enumerate(x_blocks):
         normed = work.tile([B, P], F32, name=f"normed{layer}_{c}")
@@ -54,7 +62,8 @@ def tile_ternarycreditrisknet_kernel(
         table_sb = held.tile([D, V], BF16, name="table_sb")
         nc.sync.dma_start(table_sb[:], table)
         w1_sb = held.tile([D, H], BF16, name="w1_sb")
-        nc.scalar.dma_start(w1_sb[:], w1)
+        nc.scalar.dma_start(w1_sb[:, 0:P], w1[:, 0:P])
+        nc.scalar.dma_start(w1_sb[:, P:H], w1[:, P:H])
         offsets = held.tile([P, N // 16], U16, name="offsets")
         nc.sync.dma_start(offsets[:], offs)
         b1_sb = load_columns(nc, held, b1, "b1_sb")
@@ -75,10 +84,11 @@ def tile_ternarycreditrisknet_kernel(
         ones = held.tile([1, B], F32, name="ones")
         nc.vector.memset(ones[:], 1.0)
 
-        one = held.tile([P, 1], F32, name="one")
-        nc.vector.memset(one[:], 1.0)
+        minus_half = held.tile([P, 1], F32, name="minus_half")
+        nc.vector.memset(minus_half[:], -0.5)
+
         warm = work.tile([P, 1], F32, name="warm")
-        nc.scalar.activation(warm[:], one[:], ACT.Abs_reciprocal_sqrt)
+        nc.scalar.activation(warm[:], minus_half[:], ACT.Gelu)
 
         token_sum = work.tile([P, H_BLOCKS, B], F32, name="token_sum")
         u = work.tile([P, H_BLOCKS, B], F32, name="u")
@@ -104,22 +114,22 @@ def tile_ternarycreditrisknet_kernel(
             )
 
         u_blocks = []
-        stats1 = work.tile([P, H_BLOCKS * STATS], F32, name="stats1")
+        stats1 = stats_tile(nc, work, H_BLOCKS, H, 1)
         for c in range(H_BLOCKS):
             u_ps = banks.tile([B, P], F32, name="u_ps", tag="bank")
             nc.tensor.transpose(u_ps[:], u[:, c, :], identity[:])
             nc.vector.bn_stats(stats1[:, c * STATS : (c + 1) * STATS], u_ps[:])
             u_blocks.append(u_ps[:])
-        h1 = norm_gelu(nc, work, banks, u_blocks, stats1, identity, gain1_sb, beta1_sb, 1)
+        h1 = norm_gelu(nc, work, banks, u_blocks, stats1, minus_half, identity, gain1_sb, beta1_sb, 1)
 
         v_ps = sums.tile([B, H2], F32, name="v_ps")
         nc.tensor.matmul(v_ps[:], lhsT=ones[:], rhs=b2_row[:], start=True, stop=False)
         for c in range(H_BLOCKS):
             nc.tensor.matmul(v_ps[:], lhsT=h1[:, c, :], rhs=w2_sb[:, c, :], start=False, stop=(c == H_BLOCKS - 1))
-        stats2 = work.tile([P, STATS], F32, name="stats2")
-        nc.vector.bn_stats(stats2[:], v_ps[:])
+        stats2 = stats_tile(nc, work, 1, H2, 2)
+        nc.vector.bn_stats(stats2[:, 0:STATS], v_ps[:])
         v_blocks = [v_ps[:, c * P : (c + 1) * P] for c in range(H2_BLOCKS)]
-        h2 = norm_gelu(nc, work, banks, v_blocks, stats2, identity, gain2_sb, beta2_sb, 2)
+        h2 = norm_gelu(nc, work, banks, v_blocks, stats2, minus_half, identity, gain2_sb, beta2_sb, 2)
 
         out_ps = banks.tile([NC, B], F32, name="out_ps", tag="bank")
         for c in range(H2_BLOCKS):

@@ -113,21 +113,24 @@ def tile_ternarycreditrisknet_kernel(
                 u[:, c, :], token_sum[:, c, :], ACT.Identity, bias=b1_sb[:, c : c + 1], scale=1.0 / T
             )
 
+        shared_bank = sums.tile([B, H2 + P], F32, name="shared_bank")
+        v_ps = shared_bank[:, 0:H2]
         u_blocks = []
         stats1 = stats_tile(nc, work, H_BLOCKS, H, 1)
-        for c in range(H_BLOCKS):
+        for c in range(H_BLOCKS - 1):
             u_ps = banks.tile([B, P], F32, name="u_ps", tag="bank")
-            nc.tensor.transpose(u_ps[:], u[:, c, :], identity[:])
-            nc.vector.bn_stats(stats1[:, c * STATS : (c + 1) * STATS], u_ps[:])
             u_blocks.append(u_ps[:])
+        u_blocks.append(shared_bank[:, H2 : H2 + P])
+        for c in range(H_BLOCKS):
+            nc.tensor.transpose(u_blocks[c], u[:, c, :], identity[:])
+            nc.vector.bn_stats(stats1[:, c * STATS : (c + 1) * STATS], u_blocks[c])
+        nc.tensor.matmul(v_ps, lhsT=ones[:], rhs=b2_row[:], start=True, stop=False)
         h1 = norm_gelu(nc, work, banks, u_blocks, stats1, minus_half, identity, gain1_sb, beta1_sb, 1)
 
-        v_ps = sums.tile([B, H2], F32, name="v_ps")
-        nc.tensor.matmul(v_ps[:], lhsT=ones[:], rhs=b2_row[:], start=True, stop=False)
         for c in range(H_BLOCKS):
-            nc.tensor.matmul(v_ps[:], lhsT=h1[:, c, :], rhs=w2_sb[:, c, :], start=False, stop=(c == H_BLOCKS - 1))
+            nc.tensor.matmul(v_ps, lhsT=h1[:, c, :], rhs=w2_sb[:, c, :], start=False, stop=(c == H_BLOCKS - 1))
         stats2 = stats_tile(nc, work, 1, H2, 2)
-        nc.vector.bn_stats(stats2[:, 0:STATS], v_ps[:])
+        nc.vector.bn_stats(stats2[:, 0:STATS], v_ps)
         v_blocks = [v_ps[:, c * P : (c + 1) * P] for c in range(H2_BLOCKS)]
         h2 = norm_gelu(nc, work, banks, v_blocks, stats2, minus_half, identity, gain2_sb, beta2_sb, 2)
 

@@ -71,8 +71,8 @@ def tile_ternarycreditrisknet_kernel(
         beta1_sb = load_columns(nc, held, beta1, "beta1_sb")
         w2_sb = held.tile([P, H_BLOCKS, H2], BF16, name="w2_sb")
         nc.sync.dma_start(w2_sb[:], w2.rearrange("(c p) n -> p c n", p=P))
-        b2_row = held.tile([1, H2], F32, name="b2_row")
-        nc.sync.dma_start(b2_row[:], b2.rearrange("h o -> o h"))
+        b2_rows = held.tile([B, H2], F32, name="b2_rows")
+        nc.sync.dma_start(b2_rows[:], b2.rearrange("h o -> (h o)").partition_broadcast(B))
         gain2_sb = load_columns(nc, held, gain2, "gain2_sb")
         beta2_sb = load_columns(nc, held, beta2, "beta2_sb")
         w3_sb = held.tile([P, H2_BLOCKS, NC], BF16, name="w3_sb")
@@ -81,9 +81,6 @@ def tile_ternarycreditrisknet_kernel(
 
         identity = held.tile([P, P], F32, name="identity")
         make_identity(nc, identity[:])
-        ones = held.tile([1, B], F32, name="ones")
-        nc.vector.memset(ones[:], 1.0)
-
         minus_half = held.tile([P, 1], F32, name="minus_half")
         nc.vector.memset(minus_half[:], -0.5)
 
@@ -124,7 +121,7 @@ def tile_ternarycreditrisknet_kernel(
         for c in range(H_BLOCKS):
             nc.tensor.transpose(u_blocks[c], u[:, c, :], identity[:])
             nc.vector.bn_stats(stats1[:, c * STATS : (c + 1) * STATS], u_blocks[c])
-        nc.tensor.matmul(v_ps, lhsT=ones[:], rhs=b2_row[:], start=True, stop=False)
+        nc.tensor.matmul(v_ps, lhsT=identity[:], rhs=b2_rows[:], start=True, stop=False)
         h1 = norm_gelu(nc, work, banks, u_blocks, stats1, minus_half, identity, gain1_sb, beta1_sb, 1)
 
         for c in range(H_BLOCKS):

@@ -67,6 +67,8 @@ def tile_ternarycreditrisknet_kernel(
         offsets = held.tile([P, N // 16], U16, name="offsets")
         nc.sync.dma_start(offsets[:], offs)
         b1_sb = load_columns(nc, held, b1, "b1_sb")
+        b1_last_rows = held.tile([B, P], F32, name="b1_last_rows")
+        nc.sync.dma_start(b1_last_rows[:], b1[H - P : H].rearrange("h o -> (h o)").partition_broadcast(B))
         gain1_sb = load_columns(nc, held, gain1, "gain1_sb")
         beta1_sb = load_columns(nc, held, beta1, "beta1_sb")
         w2_sb = held.tile([P, H_BLOCKS, H2], BF16, name="w2_sb")
@@ -81,6 +83,10 @@ def tile_ternarycreditrisknet_kernel(
 
         identity = held.tile([P, P], F32, name="identity")
         make_identity(nc, identity[:])
+        b1_times_t = held.tile([P, H_BLOCKS], F32, name="b1_times_t")
+        nc.vector.tensor_scalar_mul(b1_times_t[:], b1_sb[:], float(T))
+        b1_last_rows_times_t = held.tile([B, P], F32, name="b1_last_rows_times_t")
+        nc.vector.tensor_scalar_mul(b1_last_rows_times_t[:], b1_last_rows[:], float(T))
         minus_half = held.tile([P, 1], F32, name="minus_half")
         nc.vector.memset(minus_half[:], -0.5)
 
@@ -88,7 +94,7 @@ def tile_ternarycreditrisknet_kernel(
         nc.scalar.activation(warm[:], minus_half[:], ACT.Gelu)
 
         token_sum = work.tile([P, H_BLOCKS, B], F32, name="token_sum")
-        u = work.tile([P, H_BLOCKS, B], F32, name="u")
+        u = work.tile([P, H_BLOCKS - 1, B], F32, name="u")
         for c in range(H_BLOCKS):
             for piece in range(PIECES):
                 p_ps = banks.tile([P, PIECE], F32, name="p_ps", tag="bank")
@@ -106,20 +112,27 @@ def tile_ternarycreditrisknet_kernel(
                     axis=mybir.AxisListType.X,
                     op=ALU.add,
                 )
-            nc.scalar.activation(
-                u[:, c, :], token_sum[:, c, :], ACT.Identity, bias=b1_sb[:, c : c + 1], scale=1.0 / T
-            )
+            if c < H_BLOCKS - 1:
+                nc.scalar.activation(
+                    u[:, c, :], token_sum[:, c, :], ACT.Identity, bias=b1_times_t[:, c : c + 1], scale=1.0
+                )
 
         shared_bank = sums.tile([B, H2 + P], F32, name="shared_bank")
         v_ps = shared_bank[:, 0:H2]
         u_blocks = []
-        stats1 = stats_tile(nc, work, H_BLOCKS, H, 1)
+        stats1 = stats_tile(nc, work, H_BLOCKS, H * T * T, 1)
         for c in range(H_BLOCKS - 1):
             u_ps = banks.tile([B, P], F32, name="u_ps", tag="bank")
             u_blocks.append(u_ps[:])
         u_blocks.append(shared_bank[:, H2 : H2 + P])
         for c in range(H_BLOCKS):
-            nc.tensor.transpose(u_blocks[c], u[:, c, :], identity[:])
+            if c < H_BLOCKS - 1:
+                nc.tensor.transpose(u_blocks[c], u[:, c, :], identity[:])
+            else:
+                nc.tensor.matmul(u_blocks[c], lhsT=identity[:], rhs=b1_last_rows_times_t[:], start=True, stop=False)
+                nc.tensor.matmul(
+                    u_blocks[c], lhsT=token_sum[:, c, :], rhs=identity[:], is_transpose=True, start=False, stop=True
+                )
             nc.vector.bn_stats(stats1[:, c * STATS : (c + 1) * STATS], u_blocks[c])
         nc.tensor.matmul(v_ps, lhsT=identity[:], rhs=b2_rows[:], start=True, stop=False)
         h1 = norm_gelu(nc, work, banks, u_blocks, stats1, minus_half, identity, gain1_sb, beta1_sb, 1)

@@ -83,10 +83,10 @@ def tile_ternarycreditrisknet_kernel(
 
         identity = held.tile([P, P], F32, name="identity")
         make_identity(nc, identity[:])
+        identity_times_t = held.tile([P, P], F32, name="identity_times_t")
+        nc.gpsimd.tensor_scalar_mul(identity_times_t[:], identity[:], float(T))
         b1_times_t = held.tile([P, H_BLOCKS], F32, name="b1_times_t")
-        nc.vector.tensor_scalar_mul(b1_times_t[:], b1_sb[:], float(T))
-        b1_last_rows_times_t = held.tile([B, P], F32, name="b1_last_rows_times_t")
-        nc.vector.tensor_scalar_mul(b1_last_rows_times_t[:], b1_last_rows[:], float(T))
+        nc.gpsimd.tensor_scalar_mul(b1_times_t[:], b1_sb[:], float(T))
         minus_half = held.tile([P, 1], F32, name="minus_half")
         nc.vector.memset(minus_half[:], -0.5)
 
@@ -129,7 +129,7 @@ def tile_ternarycreditrisknet_kernel(
             if c < H_BLOCKS - 1:
                 nc.tensor.transpose(u_blocks[c], u[:, c, :], identity[:])
             else:
-                nc.tensor.matmul(u_blocks[c], lhsT=identity[:], rhs=b1_last_rows_times_t[:], start=True, stop=False)
+                nc.tensor.matmul(u_blocks[c], lhsT=identity_times_t[:], rhs=b1_last_rows[:], start=True, stop=False)
                 nc.tensor.matmul(
                     u_blocks[c], lhsT=token_sum[:, c, :], rhs=identity[:], is_transpose=True, start=False, stop=True
                 )

@@ -67,19 +67,19 @@ def tile_ternarycreditrisknet_kernel(
         offsets = held.tile([P, N // 16], U16, name="offsets")
         nc.sync.dma_start(offsets[:], offs)
         b1_sb = load_columns(nc, held, b1, "b1_sb")
-        b1_last_rows = held.tile([B, P], F32, name="b1_last_rows")
-        nc.sync.dma_start(b1_last_rows[:], b1[H - P : H].rearrange("h o -> (h o)").partition_broadcast(B))
         gain1_sb = load_columns(nc, held, gain1, "gain1_sb")
         beta1_sb = load_columns(nc, held, beta1, "beta1_sb")
-        w2_sb = held.tile([P, H_BLOCKS, H2], BF16, name="w2_sb")
-        nc.sync.dma_start(w2_sb[:], w2.rearrange("(c p) n -> p c n", p=P))
-        b2_rows = held.tile([B, H2], F32, name="b2_rows")
-        nc.sync.dma_start(b2_rows[:], b2.rearrange("h o -> (h o)").partition_broadcast(B))
         gain2_sb = load_columns(nc, held, gain2, "gain2_sb")
         beta2_sb = load_columns(nc, held, beta2, "beta2_sb")
-        w3_sb = held.tile([P, H2_BLOCKS, NC], BF16, name="w3_sb")
-        nc.sync.dma_start(w3_sb[:], w3.rearrange("(c p) q -> p c q", p=P))
         b3_sb = load_columns(nc, held, b3, "b3_sb")
+        b1_last_rows = held.tile([B, P], F32, name="b1_last_rows")
+        nc.scalar.dma_start(b1_last_rows[:], b1[H - P : H].rearrange("h o -> (h o)").partition_broadcast(B))
+        b2_rows = held.tile([B, H2], F32, name="b2_rows")
+        nc.scalar.dma_start(b2_rows[:], b2.rearrange("h o -> (h o)").partition_broadcast(B))
+        w2_sb = held.tile([P, H_BLOCKS, H2], BF16, name="w2_sb")
+        nc.scalar.dma_start(w2_sb[:], w2.rearrange("(c p) n -> p c n", p=P))
+        w3_sb = held.tile([P, H2_BLOCKS, NC], BF16, name="w3_sb")
+        nc.scalar.dma_start(w3_sb[:], w3.rearrange("(c p) q -> p c q", p=P))
 
         identity = held.tile([P, P], F32, name="identity")
         make_identity(nc, identity[:])

@@ -15,7 +15,7 @@ PIECES = N // PIECE
 SAMPLES = PIECE // T
 STATS = 6
 TRIPLE = 3
-BANKS = 6
+BANKS = 4
 
 FLOPS = 2 * D * H * N + 2 * H * H2 * B + 2 * H2 * NC * B
 
@@ -58,6 +58,7 @@ def tile_ternarycreditrisknet_kernel(
         tc.tile_pool(name="work", bufs=1) as work,
         tc.psum_pool(name="banks", bufs=BANKS) as banks,
         tc.psum_pool(name="sums", bufs=1) as sums,
+        tc.psum_pool(name="flips", bufs=1) as flips,
     ):
         table_sb = held.tile([D, V], BF16, name="table_sb")
         nc.sync.dma_start(table_sb[:], table)
@@ -95,6 +96,8 @@ def tile_ternarycreditrisknet_kernel(
 
         token_sum = work.tile([P, H_BLOCKS, B], F32, name="token_sum")
         u = work.tile([P, H_BLOCKS - 1, B], F32, name="u")
+        u_blocks = []
+        stats1 = stats_tile(nc, work, H_BLOCKS, H * T * T, 1)
         for c in range(H_BLOCKS):
             for piece in range(PIECES):
                 p_ps = banks.tile([P, PIECE], F32, name="p_ps", tag="bank")
@@ -116,24 +119,20 @@ def tile_ternarycreditrisknet_kernel(
                 nc.scalar.activation(
                     u[:, c, :], token_sum[:, c, :], ACT.Identity, bias=b1_times_t[:, c : c + 1], scale=1.0
                 )
+                u_ps = flips.tile([B, P], F32, name=f"u_ps{c}")
+                nc.tensor.transpose(u_ps[:], u[:, c, :], identity[:])
+                nc.vector.bn_stats(stats1[:, c * STATS : (c + 1) * STATS], u_ps[:])
+                u_blocks.append(u_ps[:])
 
         shared_bank = sums.tile([B, H2 + P], F32, name="shared_bank")
         v_ps = shared_bank[:, 0:H2]
-        u_blocks = []
-        stats1 = stats_tile(nc, work, H_BLOCKS, H * T * T, 1)
-        for c in range(H_BLOCKS - 1):
-            u_ps = banks.tile([B, P], F32, name="u_ps", tag="bank")
-            u_blocks.append(u_ps[:])
+        last = H_BLOCKS - 1
         u_blocks.append(shared_bank[:, H2 : H2 + P])
-        for c in range(H_BLOCKS):
-            if c < H_BLOCKS - 1:
-                nc.tensor.transpose(u_blocks[c], u[:, c, :], identity[:])
-            else:
-                nc.tensor.matmul(u_blocks[c], lhsT=identity_times_t[:], rhs=b1_last_rows[:], start=True, stop=False)
-                nc.tensor.matmul(
-                    u_blocks[c], lhsT=token_sum[:, c, :], rhs=identity[:], is_transpose=True, start=False, stop=True
-                )
-            nc.vector.bn_stats(stats1[:, c * STATS : (c + 1) * STATS], u_blocks[c])
+        nc.tensor.matmul(u_blocks[last], lhsT=identity_times_t[:], rhs=b1_last_rows[:], start=True, stop=False)
+        nc.tensor.matmul(
+            u_blocks[last], lhsT=token_sum[:, last, :], rhs=identity[:], is_transpose=True, start=False, stop=True
+        )
+        nc.vector.bn_stats(stats1[:, last * STATS : (last + 1) * STATS], u_blocks[last])
         nc.tensor.matmul(v_ps, lhsT=identity[:], rhs=b2_rows[:], start=True, stop=False)
         h1 = norm_gelu(nc, work, banks, u_blocks, stats1, minus_half, identity, gain1_sb, beta1_sb, 1)
 

import concourse.mybir as mybir
from concourse.masks import make_identity

BF16, F32, U16 = mybir.dt.bfloat16, mybir.dt.float32, mybir.dt.uint16
ALU = mybir.AluOpType
ACT = mybir.ActivationFunctionType

P = 128
V, D, H, H2, NC, B, T, N = 512, 128, 512, 256, 128, 128, 8, 1024
EPS = 1e-5
H_BLOCKS = H // P
H2_BLOCKS = H2 // P
PIECE = 512
PIECES = N // PIECE
SAMPLES = PIECE // T
STATS = 6
TRIPLE = 3
BANKS = 4

FLOPS = 2 * D * H * N + 2 * H * H2 * B + 2 * H2 * NC * B


def load_columns(nc, pool, vector, name):
    columns = pool.tile([P, vector.shape[0] // P], F32, name=name)
    with nc.allow_non_contiguous_dma(reason="4-byte elements, one to a partition"):
        nc.sync.dma_start(columns[:], vector.rearrange("(c p) o -> p (c o)", p=P))
    return columns


def stats_tile(nc, work, chunks, features, layer):
    stats = work.tile([P, chunks * STATS + TRIPLE], F32, name=f"stats{layer}")
    nc.vector.memset(stats[:, chunks * STATS : chunks * STATS + 2], 0.0)
    nc.vector.memset(stats[:, chunks * STATS + 2 : chunks * STATS + TRIPLE], features * EPS)
    return stats


def norm_gelu(nc, work, banks, x_blocks, stats, minus_half, identity, gain, beta, layer):
    mean_var = work.tile([P, 2], F32, name=f"mean_var{layer}")
    nc.vector.bn_aggr(mean_var[:], stats[:])
    rstd = work.tile([P, 1], F32, name=f"rstd{layer}")
    nc.gpsimd.tensor_tensor(rstd[:], mean_var[:, 1:2], minus_half[:], ALU.pow)
    h = work.tile([P, len(x_blocks), B], BF16, name=f"h{layer}")
    for c, x_block in enumerate(x_blocks):
        normed = work.tile([B, P], F32, name=f"normed{layer}_{c}")
        nc.vector.tensor_scalar(normed[:], x_block, mean_var[:, 0:1], rstd[:], ALU.subtract, ALU.mult)
        flipped = banks.tile([P, B], F32, name="flipped", tag="bank")
        nc.tensor.transpose(flipped[:], normed[:], identity[:])
        nc.scalar.activation(h[:, c, :], flipped[:], ACT.Gelu, bias=beta[:, c : c + 1], scale=gain[:, c : c + 1])
    return h


def tile_ternarycreditrisknet_kernel(
    tc, table, w1, b1, gain1, beta1, w2, b2, gain2, beta2, w3, b3, offs, out
):
    nc = tc.nc
    with (
        tc.tile_pool(name="held", bufs=1) as held,
        tc.tile_pool(name="work", bufs=1) as work,
        tc.psum_pool(name="banks", bufs=BANKS) as banks,
        tc.psum_pool(name="sums", bufs=1) as sums,
        tc.psum_pool(name="flips", bufs=1) as flips,
    ):
        table_sb = held.tile([D, V], BF16, name="table_sb")
        nc.sync.dma_start(table_sb[:], table)
        w1_sb = held.tile([D, H], BF16, name="w1_sb")
        nc.scalar.dma_start(w1_sb[:, 0:P], w1[:, 0:P])
        nc.scalar.dma_start(w1_sb[:, P:H], w1[:, P:H])
        offsets = held.tile([P, N // 16], U16, name="offsets")
        nc.sync.dma_start(offsets[:], offs)
        b1_sb = load_columns(nc, held, b1, "b1_sb")
        gain1_sb = load_columns(nc, held, gain1, "gain1_sb")
        beta1_sb = load_columns(nc, held, beta1, "beta1_sb")
        gain2_sb = load_columns(nc, held, gain2, "gain2_sb")
        beta2_sb = load_columns(nc, held, beta2, "beta2_sb")
        b3_sb = load_columns(nc, held, b3, "b3_sb")
        b1_last_rows = held.tile([B, P], F32, name="b1_last_rows")
        nc.scalar.dma_start(b1_last_rows[:], b1[H - P : H].rearrange("h o -> (h o)").partition_broadcast(B))
        b2_rows = held.tile([B, H2], F32, name="b2_rows")
        nc.scalar.dma_start(b2_rows[:], b2.rearrange("h o -> (h o)").partition_broadcast(B))
        w2_sb = held.tile([P, H_BLOCKS, H2], BF16, name="w2_sb")
        nc.scalar.dma_start(w2_sb[:], w2.rearrange("(c p) n -> p c n", p=P))
        w3_sb = held.tile([P, H2_BLOCKS, NC], BF16, name="w3_sb")
        nc.scalar.dma_start(w3_sb[:], w3.rearrange("(c p) q -> p c q", p=P))

        identity = held.tile([P, P], F32, name="identity")
        make_identity(nc, identity[:])
        identity_times_t = held.tile([P, P], F32, name="identity_times_t")
        nc.gpsimd.tensor_scalar_mul(identity_times_t[:], identity[:], float(T))
        b1_times_t = held.tile([P, H_BLOCKS], F32, name="b1_times_t")
        nc.gpsimd.tensor_scalar_mul(b1_times_t[:], b1_sb[:], float(T))
        minus_half = held.tile([P, 1], F32, name="minus_half")
        nc.vector.memset(minus_half[:], -0.5)

        warm = work.tile([P, 1], F32, name="warm")
        nc.scalar.activation(warm[:], minus_half[:], ACT.Gelu)

        token_sum = work.tile([P, H_BLOCKS, B], F32, name="token_sum")
        u = work.tile([P, H_BLOCKS - 1, B], F32, name="u")
        u_blocks = []
        stats1 = stats_tile(nc, work, H_BLOCKS, H * T * T, 1)
        for c in range(H_BLOCKS):
            for piece in range(PIECES):
                p_ps = banks.tile([P, PIECE], F32, name="p_ps", tag="bank")
                piece_offsets = offsets[:, piece * (PIECE // 16) : (piece + 1) * (PIECE // 16)]
                nc.tensor.matmul(
                    p_ps[:],
                    lhsT=w1_sb[:, c * P : (c + 1) * P],
                    rhs=table_sb[:].indirect(piece_offsets),
                    start=True,
                    stop=True,
                )
                nc.vector.tensor_reduce(
                    out=token_sum[:, c, piece * SAMPLES : (piece + 1) * SAMPLES],
                    in_=p_ps[:].rearrange("p (i t) -> p i t", t=T),
                    axis=mybir.AxisListType.X,
                    op=ALU.add,
                )
            if c < H_BLOCKS - 1:
                nc.scalar.activation(
                    u[:, c, :], token_sum[:, c, :], ACT.Identity, bias=b1_times_t[:, c : c + 1], scale=1.0
                )
                u_ps = flips.tile([B, P], F32, name=f"u_ps{c}")
                nc.tensor.transpose(u_ps[:], u[:, c, :], identity[:])
                nc.vector.bn_stats(stats1[:, c * STATS : (c + 1) * STATS], u_ps[:])
                u_blocks.append(u_ps[:])

        shared_bank = sums.tile([B, H2 + P], F32, name="shared_bank")
        v_ps = shared_bank[:, 0:H2]
        last = H_BLOCKS - 1
        u_blocks.append(shared_bank[:, H2 : H2 + P])
        nc.tensor.matmul(u_blocks[last], lhsT=identity_times_t[:], rhs=b1_last_rows[:], start=True, stop=False)
        nc.tensor.matmul(
            u_blocks[last], lhsT=token_sum[:, last, :], rhs=identity[:], is_transpose=True, start=False, stop=True
        )
        nc.vector.bn_stats(stats1[:, last * STATS : (last + 1) * STATS], u_blocks[last])
        nc.tensor.matmul(v_ps, lhsT=identity[:], rhs=b2_rows[:], start=True, stop=False)
        h1 = norm_gelu(nc, work, banks, u_blocks, stats1, minus_half, identity, gain1_sb, beta1_sb, 1)

        for c in range(H_BLOCKS):
            nc.tensor.matmul(v_ps, lhsT=h1[:, c, :], rhs=w2_sb[:, c, :], start=False, stop=(c == H_BLOCKS - 1))
        stats2 = stats_tile(nc, work, 1, H2, 2)
        nc.vector.bn_stats(stats2[:, 0:STATS], v_ps)
        v_blocks = [v_ps[:, c * P : (c + 1) * P] for c in range(H2_BLOCKS)]
        h2 = norm_gelu(nc, work, banks, v_blocks, stats2, minus_half, identity, gain2_sb, beta2_sb, 2)

        out_ps = banks.tile([NC, B], F32, name="out_ps", tag="bank")
        for c in range(H2_BLOCKS):
            nc.tensor.matmul(out_ps[:], lhsT=w3_sb[:, c, :], rhs=h2[:, c, :], start=(c == 0), stop=(c == H2_BLOCKS - 1))
        out_sb = work.tile([NC, B], F32, name="out_sb")
        nc.vector.tensor_scalar_add(out_sb[:], out_ps[:], b3_sb[:])
        nc.sync.dma_start(out, out_sb[:])
